import numpy as np
import ml_dtypes


def mxq(x, axis, fmt="e4m3"):
    dtype, down = {"e4m3": (ml_dtypes.float8_e4m3fn, 7), "e5m2": (ml_dtypes.float8_e5m2, 14)}[fmt]
    v = np.moveaxis(np.asarray(x, np.float32).astype(ml_dtypes.bfloat16).astype(np.float64), axis, -1)
    blocks = v.reshape(v.shape[:-1] + (-1, 32))
    amax = np.abs(blocks).max(-1, keepdims=True)
    byte = np.maximum(np.where(amax > 0, np.frexp(amax)[1] - 1 + 127, 0) - down, 1)
    scale = np.exp2(byte - 127.0)
    codes = (blocks / scale).astype(np.float32).astype(dtype).astype(np.float64)
    return np.moveaxis((codes * scale).reshape(v.shape), -1, axis)


WIDE = False


def mx_kscale(k):
    if not WIDE:
        return np.ones(k)
    levels = np.array([10, -10, 5, -5, 0])
    if k % 512:
        return np.exp2(np.random.permutation(np.resize(levels, k // 32))).repeat(32)
    a = np.empty((k // 512, 16))
    for p in range(k // 512):
        a[p, :8] = np.random.permutation(np.resize(levels, 8))
        for g in range(8):
            far = levels[np.abs(levels - a[p, g]) >= 10]
            a[p, g + 8] = far[np.random.randint(len(far))]
    return np.exp2(a.ravel()).repeat(32)


BF16 = ml_dtypes.bfloat16


def bf(x):
    return np.asarray(x, np.float32).astype(BF16)


def f64(x):
    return np.asarray(x).astype(np.float64)


B, S, H, HD = 4, 2048, 4, 128
DIM = H * HD


def setup_inputs():
    s, t = mx_kscale(DIM), mx_kscale(DIM)
    return {"x": bf(np.random.standard_normal((B, S, DIM)) * 2.0 * s),
            "y_norm": bf(np.random.standard_normal((B, S, DIM))),
            "wg_w": bf(np.random.standard_normal((DIM, DIM)) * 0.5 / np.sqrt(DIM) / s[:, None] * t),
            "wo_w": bf(np.random.standard_normal((DIM, DIM)) * 1.5 / np.sqrt(DIM) / t[:, None])}


def reference(x, y_norm, wg_w, wo_w):
    g = np.maximum(mxq(f64(x), 2, "e4m3") @ mxq(f64(wg_w), 0, "e4m3"), 0.0)
    h = g * f64(y_norm)
    return mxq(h, 2, "e4m3") @ mxq(f64(wo_w), 0, "e4m3")

@@ -1,0 +1,226 @@
+from contextlib import ExitStack
+
+import concourse.mybir as mybir
+from concourse.masks import make_identity
+
+BF16 = mybir.dt.bfloat16
+F32 = mybir.dt.float32
+U32 = mybir.dt.uint32
+U8 = mybir.dt.uint8
+FP8X4 = mybir.dt.float8_e4m3fn_x4
+
+P = 128
+PACK = 4
+D = P * PACK
+WORDS = D // 2
+TOKENS = 4 * 2048
+
+SUBS = 8
+CHUNK = SUBS * P
+CHUNKS = TOKENS // CHUNK
+ROUND_SUBS = 2
+ROUND_COLS = ROUND_SUBS * D
+ROUNDS = TOKENS // (ROUND_SUBS * P)
+CHUNK_ROUNDS = SUBS // ROUND_SUBS
+LOADS_AHEAD = 3
+
+FIRST_MATMUL_LAG = 1
+QUANTISE_H_LAG = 2
+SECOND_MATMUL_LAG = 3
+
+VECTOR_OUT_SHARE = 8
+
+FLOPS = 2 * 2 * TOKENS * D * D
+
+
+def tile_multiscaleretention_pb_t_kernel(tc, x, y_norm, wg_w, wo_w, out):
+    nc = tc.nc
+    x_rows = x.flatten_outer_dims()
+    y_rows = y_norm.flatten_outer_dims()
+    out_rows = out.flatten_outer_dims()
+
+    def chunk_view(rows, c):
+        return rows[c * CHUNK : (c + 1) * CHUNK, :].rearrange("(p s) d -> p (s d)", s=SUBS)
+
+    with ExitStack() as ctx:
+        ctx.enter_context(tc.manual_schedule())
+        const = ctx.enter_context(tc.tile_pool(name="const", bufs=1))
+        loads = ctx.enter_context(tc.tile_pool(name="loads", bufs=LOADS_AHEAD + 1))
+        work = ctx.enter_context(tc.tile_pool(name="work", bufs=3))
+        stores = ctx.enter_context(tc.tile_pool(name="stores", bufs=10))
+        psum_t = ctx.enter_context(tc.psum_pool(name="psum_t", bufs=1))
+        psum_mx = ctx.enter_context(tc.psum_pool(name="psum_mx", bufs=3))
+
+        x_chunks = {}
+        y_chunks = {}
+
+        def load_rounds(c, first_round, rounds):
+            cols = slice(first_round * ROUND_COLS, (first_round + rounds) * ROUND_COLS)
+            nc.sync.dma_start(out=x_chunks[c][:, cols], in_=chunk_view(x_rows, c)[:, cols])
+            nc.sync.dma_start(out=y_chunks[c][:, cols], in_=chunk_view(y_rows, c)[:, cols])
+
+        def load_weight(w, name):
+            raw = const.tile([P, PACK, D], BF16, name=name)
+            nc.sync.dma_start(out=raw[:], in_=w.rearrange("(p t) c -> p t c", t=PACK))
+            return raw
+
+        weights_raw = {}
+
+        def load_chunk(c):
+            x_sb = loads.tile([P, SUBS * D], BF16, tag="x")
+            y_sb = loads.tile([P, SUBS * D], BF16, tag="y")
+            x_chunks[c] = x_sb
+            y_chunks[c] = y_sb
+            rounds = min(CHUNK_ROUNDS, 2**c)
+            for first_round in range(0, CHUNK_ROUNDS, rounds):
+                load_rounds(c, first_round, rounds)
+                if c == 0 and first_round == 0:
+                    weights_raw["wo"] = load_weight(wo_w, "wo_raw")
+
+        weights_raw["wg"] = load_weight(wg_w, "wg_raw")
+        for c in range(LOADS_AHEAD):
+            load_chunk(c)
+
+        ident = const.tile([P, P], F32)
+        make_identity(nc, ident[:])
+
+        def quantise_weight(grouped, name):
+            codes = const.tile([P, D], U32, name=name + "_codes", align_bytes=64)
+            scales = const.tile([P, D], U8, name=name + "_scales", align_bytes=64)
+            nc.vector.quantize_mx(out=codes[:].bitcast(FP8X4), scales=scales[:], in_=grouped[:])
+            return codes, scales
+
+        wg_grouped = const.tile([P, D * PACK], BF16, align_bytes=64)
+        wg_sorted = wg_grouped[:].rearrange("p (t q j) -> p t q j", t=PACK, j=PACK)
+        wg_cols = weights_raw["wg"][:].rearrange("p j (q t) -> p t q j", t=PACK)
+        for t in range(PACK):
+            nc.vector.tensor_copy(out=wg_sorted[:, t], in_=wg_cols[:, t])
+        wg_codes, wg_scales = quantise_weight(wg_grouped, "wg")
+
+        wo_mx = {}
+
+        def prepare_wo():
+            wo_grouped = const.tile([P, D * PACK], BF16, align_bytes=64)
+            nc.vector.tensor_copy(
+                out=wo_grouped[:].rearrange("p (c t) -> p c t", t=PACK),
+                in_=weights_raw["wo"][:].rearrange("p t c -> p c t"),
+            )
+            wo_mx["codes"], wo_mx["scales"] = quantise_weight(wo_grouped, "wo")
+
+        x_grouped = {}
+        y_grouped = {}
+        x_mx = {}
+        g_banks = {}
+        h_grouped = {}
+        h_mx = {}
+        out_banks = {}
+
+        def transpose_round(r):
+            c, first_sub = r // CHUNK_ROUNDS, (r % CHUNK_ROUNDS) * ROUND_SUBS
+            banks = []
+            for chunks, tag in ((x_chunks, "xT"), (y_chunks, "yT")):
+                words = chunks[c][:].bitcast(F32)
+                bank = psum_t.tile([P, ROUND_SUBS, 2, P], F32, tag=tag)
+                for s in range(ROUND_SUBS):
+                    for u in range(2):
+                        start = (first_sub + s) * WORDS
+                        nc.tensor.transpose(
+                            bank[:, s, u, :], words[:, start + u : start + WORDS : 2], ident[:]
+                        )
+                banks.append(bank)
+            for bank, grouped, tag in zip(banks, (x_grouped, y_grouped), ("x_grouped", "y_grouped")):
+                tile_bf16 = work.tile([P, ROUND_COLS], BF16, tag=tag, align_bytes=64)
+                nc.scalar.copy(
+                    out=tile_bf16[:].bitcast(F32).rearrange("p (s r u) -> p s r u", s=ROUND_SUBS, u=2),
+                    in_=bank[:].rearrange("p s u r -> p s r u"),
+                )
+                grouped[r] = tile_bf16
+
+        def quantise_round(grouped, name):
+            codes = work.tile([P, ROUND_SUBS * P], U32, tag=name + "_codes", align_bytes=64)
+            scales = work.tile([P, ROUND_SUBS * P], U8, tag=name + "_scales", align_bytes=64)
+            nc.vector.quantize_mx(out=codes[:].bitcast(FP8X4), scales=scales[:], in_=grouped[:])
+            return codes, scales
+
+        def first_matmul_round(r):
+            codes, scales = x_mx[r]
+            g_banks[r] = []
+            for s in range(ROUND_SUBS):
+                tokens = slice(s * P, (s + 1) * P)
+                g_bank = psum_mx.tile([P, PACK, P], F32, tag="g")
+                for t in range(PACK):
+                    cols = slice(t * P, (t + 1) * P)
+                    nc.tensor.matmul_mx(
+                        out=g_bank[:, t, :],
+                        lhsT=wg_codes[:, cols].bitcast(FP8X4),
+                        lhsT_scale=wg_scales[:, cols],
+                        rhs=codes[:, tokens].bitcast(FP8X4),
+                        rhs_scale=scales[:, tokens],
+                        start=True,
+                        stop=True,
+                    )
+                g_banks[r].append(g_bank)
+
+        def gate_round(r):
+            h_bf16 = work.tile([P, ROUND_COLS], BF16, tag="h_grouped", align_bytes=64)
+            for s in range(ROUND_SUBS):
+                span = slice(s * D, (s + 1) * D)
+                nc.vector.scalar_tensor_tensor(
+                    out=h_bf16[:, span].rearrange("p (r t) -> p r t", t=PACK),
+                    in0=g_banks[r][s][:].rearrange("p t r -> p r t"),
+                    scalar=0.0,
+                    in1=y_grouped[r][:, span].rearrange("p (r t) -> p r t", t=PACK),
+                    op0=mybir.AluOpType.max,
+                    op1=mybir.AluOpType.mult,
+                )
+            h_grouped[r] = h_bf16
+
+        def second_matmul_round(r):
+            codes, scales = h_mx[r]
+            out_banks[r] = []
+            for s in range(ROUND_SUBS):
+                tokens = slice(s * P, (s + 1) * P)
+                out_bank = psum_mx.tile([P, D], F32, tag="out")
+                nc.tensor.matmul_mx(
+                    out=out_bank[:],
+                    lhsT=codes[:, tokens].bitcast(FP8X4),
+                    lhsT_scale=scales[:, tokens],
+                    rhs=wo_mx["codes"][:].bitcast(FP8X4),
+                    rhs_scale=wo_mx["scales"][:],
+                    start=True,
+                    stop=True,
+                )
+                out_banks[r].append(out_bank)
+
+        def store_round(r):
+            out_sb = stores.tile([P, ROUND_COLS], F32)
+            for s in range(ROUND_SUBS):
+                span = slice(s * D, (s + 1) * D)
+                if (r * ROUND_SUBS + s) % VECTOR_OUT_SHARE == VECTOR_OUT_SHARE - 1:
+                    nc.vector.tensor_copy(out=out_sb[:, span], in_=out_banks[r][s][:])
+                else:
+                    nc.scalar.copy(out=out_sb[:, span], in_=out_banks[r][s][:])
+            first = (r % CHUNK_ROUNDS) * ROUND_COLS
+            nc.sync.dma_start(
+                out=chunk_view(out_rows, r // CHUNK_ROUNDS)[:, first : first + ROUND_COLS],
+                in_=out_sb[:],
+            )
+
+        for i in range(ROUNDS + SECOND_MATMUL_LAG):
+            if i % CHUNK_ROUNDS == 0 and i // CHUNK_ROUNDS + LOADS_AHEAD < CHUNKS:
+                load_chunk(i // CHUNK_ROUNDS + LOADS_AHEAD)
+            if i < ROUNDS:
+                transpose_round(i)
+                x_mx[i] = quantise_round(x_grouped[i], "x")
+            if i == 0:
+                prepare_wo()
+            if 0 <= i - QUANTISE_H_LAG < ROUNDS:
+                h_mx[i - QUANTISE_H_LAG] = quantise_round(h_grouped[i - QUANTISE_H_LAG], "h")
+            if 0 <= i - SECOND_MATMUL_LAG < ROUNDS:
+                second_matmul_round(i - SECOND_MATMUL_LAG)
+            if 0 <= i - FIRST_MATMUL_LAG < ROUNDS:
+                first_matmul_round(i - FIRST_MATMUL_LAG)
+            if 0 <= i - SECOND_MATMUL_LAG < ROUNDS:
+                store_round(i - SECOND_MATMUL_LAG)
+            if 0 <= i - FIRST_MATMUL_LAG < ROUNDS:
+                gate_round(i - FIRST_MATMUL_LAG)

@@ -25,7 +25,7 @@ CHUNK_ROUNDS = SUBS // ROUND_SUBS
 LOADS_AHEAD = 3
 
 FIRST_MATMUL_LAG = 1
-QUANTISE_H_LAG = 2
+TRANSPOSE_H_LAG = 2
 SECOND_MATMUL_LAG = 3
 
 VECTOR_OUT_SHARE = 8
@@ -91,10 +91,10 @@ def tile_multiscaleretention_pb_t_kernel(tc, x, y_norm, wg_w, wo_w, out):
             return codes, scales
 
         wg_grouped = const.tile([P, D * PACK], BF16, align_bytes=64)
-        wg_sorted = wg_grouped[:].rearrange("p (t q j) -> p t q j", t=PACK, j=PACK)
-        wg_cols = weights_raw["wg"][:].rearrange("p j (q t) -> p t q j", t=PACK)
-        for t in range(PACK):
-            nc.vector.tensor_copy(out=wg_sorted[:, t], in_=wg_cols[:, t])
+        wg_sorted = wg_grouped[:].rearrange("p (u q e t) -> p u q e t", u=2, e=2, t=PACK)
+        wg_cols = weights_raw["wg"][:].rearrange("p t (q u e) -> p u q e t", u=2, e=2)
+        for u in range(2):
+            nc.vector.tensor_copy(out=wg_sorted[:, u], in_=wg_cols[:, u])
         wg_codes, wg_scales = quantise_weight(wg_grouped, "wg")
 
         wo_mx = {}
@@ -108,33 +108,41 @@ def tile_multiscaleretention_pb_t_kernel(tc, x, y_norm, wg_w, wo_w, out):
             wo_mx["codes"], wo_mx["scales"] = quantise_weight(wo_grouped, "wo")
 
         x_grouped = {}
-        y_grouped = {}
         x_mx = {}
         g_banks = {}
+        h_rows = {}
         h_grouped = {}
         h_mx = {}
         out_banks = {}
 
-        def transpose_round(r):
+        def transpose_x_round(r):
             c, first_sub = r // CHUNK_ROUNDS, (r % CHUNK_ROUNDS) * ROUND_SUBS
-            banks = []
-            for chunks, tag in ((x_chunks, "xT"), (y_chunks, "yT")):
-                words = chunks[c][:].bitcast(F32)
-                bank = psum_t.tile([P, ROUND_SUBS, 2, P], F32, tag=tag)
-                for s in range(ROUND_SUBS):
-                    for u in range(2):
-                        start = (first_sub + s) * WORDS
-                        nc.tensor.transpose(
-                            bank[:, s, u, :], words[:, start + u : start + WORDS : 2], ident[:]
-                        )
-                banks.append(bank)
-            for bank, grouped, tag in zip(banks, (x_grouped, y_grouped), ("x_grouped", "y_grouped")):
-                tile_bf16 = work.tile([P, ROUND_COLS], BF16, tag=tag, align_bytes=64)
-                nc.scalar.copy(
-                    out=tile_bf16[:].bitcast(F32).rearrange("p (s r u) -> p s r u", s=ROUND_SUBS, u=2),
-                    in_=bank[:].rearrange("p s u r -> p s r u"),
-                )
-                grouped[r] = tile_bf16
+            words = x_chunks[c][:].bitcast(F32)
+            bank = psum_t.tile([P, ROUND_SUBS, 2, P], F32, tag="xT")
+            for s in range(ROUND_SUBS):
+                for u in range(2):
+                    start = (first_sub + s) * WORDS
+                    nc.tensor.transpose(
+                        bank[:, s, u, :], words[:, start + u : start + WORDS : 2], ident[:]
+                    )
+            return bank
+
+        def transpose_h_round(r):
+            words = h_rows[r][:].bitcast(F32)
+            bank = psum_t.tile([P, ROUND_SUBS, 2, P], F32, tag="hT")
+            for s in range(ROUND_SUBS):
+                for u in range(2):
+                    start = (u * ROUND_SUBS + s) * P
+                    nc.tensor.transpose(bank[:, s, u, :], words[:, start : start + P], ident[:])
+            return bank
+
+        def group_round(bank, tag):
+            tile_bf16 = work.tile([P, ROUND_COLS], BF16, tag=tag, align_bytes=64)
+            nc.scalar.copy(
+                out=tile_bf16[:].bitcast(F32).rearrange("p (s r u) -> p s r u", s=ROUND_SUBS, u=2),
+                in_=bank[:].rearrange("p s u r -> p s r u"),
+            )
+            return tile_bf16
 
         def quantise_round(grouped, name):
             codes = work.tile([P, ROUND_SUBS * P], U32, tag=name + "_codes", align_bytes=64)
@@ -145,44 +153,30 @@ def tile_multiscaleretention_pb_t_kernel(tc, x, y_norm, wg_w, wo_w, out):
         def first_matmul_round(r):
             codes, scales = x_mx[r]
             g_banks[r] = []
-            for s in range(ROUND_SUBS):
-                tokens = slice(s * P, (s + 1) * P)
-                g_bank = psum_mx.tile([P, PACK, P], F32, tag="g")
-                for t in range(PACK):
-                    cols = slice(t * P, (t + 1) * P)
+            for u in range(2):
+                cols = slice(u * WORDS, (u + 1) * WORDS)
+                bank = psum_mx.tile([P, ROUND_SUBS, WORDS], F32, tag="g")
+                for s in range(ROUND_SUBS):
+                    tokens = slice(s * P, (s + 1) * P)
                     nc.tensor.matmul_mx(
-                        out=g_bank[:, t, :],
-                        lhsT=wg_codes[:, cols].bitcast(FP8X4),
-                        lhsT_scale=wg_scales[:, cols],
-                        rhs=codes[:, tokens].bitcast(FP8X4),
-                        rhs_scale=scales[:, tokens],
+                        out=bank[:, s, :],
+                        lhsT=codes[:, tokens].bitcast(FP8X4),
+                        lhsT_scale=scales[:, tokens],
+                        rhs=wg_codes[:, cols].bitcast(FP8X4),
+                        rhs_scale=wg_scales[:, cols],
                         start=True,
                         stop=True,
                     )
-                g_banks[r].append(g_bank)
-
-        def gate_round(r):
-            h_bf16 = work.tile([P, ROUND_COLS], BF16, tag="h_grouped", align_bytes=64)
-            for s in range(ROUND_SUBS):
-                span = slice(s * D, (s + 1) * D)
-                nc.vector.scalar_tensor_tensor(
-                    out=h_bf16[:, span].rearrange("p (r t) -> p r t", t=PACK),
-                    in0=g_banks[r][s][:].rearrange("p t r -> p r t"),
-                    scalar=0.0,
-                    in1=y_grouped[r][:, span].rearrange("p (r t) -> p r t", t=PACK),
-                    op0=mybir.AluOpType.max,
-                    op1=mybir.AluOpType.mult,
-                )
-            h_grouped[r] = h_bf16
+                g_banks[r].append(bank)
 
         def second_matmul_round(r):
             codes, scales = h_mx[r]
             out_banks[r] = []
             for s in range(ROUND_SUBS):
                 tokens = slice(s * P, (s + 1) * P)
-                out_bank = psum_mx.tile([P, D], F32, tag="out")
+                bank = psum_mx.tile([P, D], F32, tag="out")
                 nc.tensor.matmul_mx(
-                    out=out_bank[:],
+                    out=bank[:],
                     lhsT=codes[:, tokens].bitcast(FP8X4),
                     lhsT_scale=scales[:, tokens],
                     rhs=wo_mx["codes"][:].bitcast(FP8X4),
@@ -190,7 +184,23 @@ def tile_multiscaleretention_pb_t_kernel(tc, x, y_norm, wg_w, wo_w, out):
                     start=True,
                     stop=True,
                 )
-                out_banks[r].append(out_bank)
+                out_banks[r].append(bank)
+
+        def gate_round(r):
+            c, first = r // CHUNK_ROUNDS, (r % CHUNK_ROUNDS) * ROUND_COLS
+            y_words = y_chunks[c][:, first : first + ROUND_COLS].rearrange("p (q u e) -> p u q e", u=2, e=2)
+            h_bf16 = work.tile([P, ROUND_COLS], BF16, tag="h_rows", align_bytes=64)
+            h_words = h_bf16[:].rearrange("p (u q e) -> p u q e", u=2, e=2)
+            for u in range(2):
+                nc.vector.scalar_tensor_tensor(
+                    out=h_words[:, u],
+                    in0=g_banks[r][u][:].rearrange("p s (q e) -> p (s q) e", e=2),
+                    scalar=0.0,
+                    in1=y_words[:, u],
+                    op0=mybir.AluOpType.max,
+                    op1=mybir.AluOpType.mult,
+                )
+            h_rows[r] = h_bf16
 
         def store_round(r):
             out_sb = stores.tile([P, ROUND_COLS], F32)
@@ -209,18 +219,28 @@ def tile_multiscaleretention_pb_t_kernel(tc, x, y_norm, wg_w, wo_w, out):
         for i in range(ROUNDS + SECOND_MATMUL_LAG):
             if i % CHUNK_ROUNDS == 0 and i // CHUNK_ROUNDS + LOADS_AHEAD < CHUNKS:
                 load_chunk(i // CHUNK_ROUNDS + LOADS_AHEAD)
-            if i < ROUNDS:
-                transpose_round(i)
-                x_mx[i] = quantise_round(x_grouped[i], "x")
-            if i == 0:
+            first_r = i - FIRST_MATMUL_LAG
+            h_r = i - TRANSPOSE_H_LAG
+            second_r = i - SECOND_MATMUL_LAG
+            if 0 <= first_r < ROUNDS:
+                x_mx[first_r] = quantise_round(x_grouped[first_r], "x")
+            if i == 1:
                 prepare_wo()
-            if 0 <= i - QUANTISE_H_LAG < ROUNDS:
-                h_mx[i - QUANTISE_H_LAG] = quantise_round(h_grouped[i - QUANTISE_H_LAG], "h")
-            if 0 <= i - SECOND_MATMUL_LAG < ROUNDS:
-                second_matmul_round(i - SECOND_MATMUL_LAG)
-            if 0 <= i - FIRST_MATMUL_LAG < ROUNDS:
-                first_matmul_round(i - FIRST_MATMUL_LAG)
-            if 0 <= i - SECOND_MATMUL_LAG < ROUNDS:
-                store_round(i - SECOND_MATMUL_LAG)
-            if 0 <= i - FIRST_MATMUL_LAG < ROUNDS:
-                gate_round(i - FIRST_MATMUL_LAG)
+            if 0 <= second_r < ROUNDS:
+                h_mx[second_r] = quantise_round(h_grouped[second_r], "h")
+            if i < ROUNDS:
+                x_bank = transpose_x_round(i)
+            if 0 <= h_r < ROUNDS:
+                h_bank = transpose_h_round(h_r)
+            if i < ROUNDS:
+                x_grouped[i] = group_round(x_bank, "x_grouped")
+            if 0 <= h_r < ROUNDS:
+                h_grouped[h_r] = group_round(h_bank, "h_grouped")
+            if 0 <= first_r < ROUNDS:
+                first_matmul_round(first_r)
+            if 0 <= second_r < ROUNDS:
+                second_matmul_round(second_r)
+            if 0 <= first_r < ROUNDS:
+                gate_round(first_r)
+            if 0 <= second_r < ROUNDS:
+                store_round(second_r)

@@ -24,11 +24,13 @@ ROUNDS = TOKENS // (ROUND_SUBS * P)
 CHUNK_ROUNDS = SUBS // ROUND_SUBS
 LOADS_AHEAD = 3
 
-FIRST_MATMUL_LAG = 1
-TRANSPOSE_H_LAG = 2
-SECOND_MATMUL_LAG = 3
+QUANTISE_X_LAG = 1
+FIRST_MATMUL_LAG = 2
+TRANSPOSE_H_LAG = 4
+QUANTISE_H_LAG = 5
+SECOND_MATMUL_LAG = 6
 
-VECTOR_OUT_SHARE = 8
+VECTOR_OUT_SHARE = 4
 
 FLOPS = 2 * 2 * TOKENS * D * D
 
@@ -46,7 +48,7 @@ def tile_multiscaleretention_pb_t_kernel(tc, x, y_norm, wg_w, wo_w, out):
         ctx.enter_context(tc.manual_schedule())
         const = ctx.enter_context(tc.tile_pool(name="const", bufs=1))
         loads = ctx.enter_context(tc.tile_pool(name="loads", bufs=LOADS_AHEAD + 1))
-        work = ctx.enter_context(tc.tile_pool(name="work", bufs=3))
+        work = ctx.enter_context(tc.tile_pool(name="work", bufs=4))
         stores = ctx.enter_context(tc.tile_pool(name="stores", bufs=10))
         psum_t = ctx.enter_context(tc.psum_pool(name="psum_t", bufs=1))
         psum_mx = ctx.enter_context(tc.psum_pool(name="psum_mx", bufs=3))
@@ -219,15 +221,17 @@ def tile_multiscaleretention_pb_t_kernel(tc, x, y_norm, wg_w, wo_w, out):
         for i in range(ROUNDS + SECOND_MATMUL_LAG):
             if i % CHUNK_ROUNDS == 0 and i // CHUNK_ROUNDS + LOADS_AHEAD < CHUNKS:
                 load_chunk(i // CHUNK_ROUNDS + LOADS_AHEAD)
+            quantise_x_r = i - QUANTISE_X_LAG
             first_r = i - FIRST_MATMUL_LAG
             h_r = i - TRANSPOSE_H_LAG
+            quantise_h_r = i - QUANTISE_H_LAG
             second_r = i - SECOND_MATMUL_LAG
-            if 0 <= first_r < ROUNDS:
-                x_mx[first_r] = quantise_round(x_grouped[first_r], "x")
-            if i == 1:
+            if 0 <= quantise_x_r < ROUNDS:
+                x_mx[quantise_x_r] = quantise_round(x_grouped[quantise_x_r], "x")
+            if i == FIRST_MATMUL_LAG:
                 prepare_wo()
-            if 0 <= second_r < ROUNDS:
-                h_mx[second_r] = quantise_round(h_grouped[second_r], "h")
+            if 0 <= quantise_h_r < ROUNDS:
+                h_mx[quantise_h_r] = quantise_round(h_grouped[quantise_h_r], "h")
             if i < ROUNDS:
                 x_bank = transpose_x_round(i)
             if 0 <= h_r < ROUNDS:

@@ -20,15 +20,16 @@ CHUNK = SUBS * P
 CHUNKS = TOKENS // CHUNK
 ROUND_SUBS = 2
 ROUND_COLS = ROUND_SUBS * D
+ROUND_WORDS = ROUND_SUBS * P
 ROUNDS = TOKENS // (ROUND_SUBS * P)
 CHUNK_ROUNDS = SUBS // ROUND_SUBS
 LOADS_AHEAD = 3
 
-QUANTISE_X_LAG = 1
+QUANTISE_LAG = 1
 FIRST_MATMUL_LAG = 2
 TRANSPOSE_H_LAG = 4
-QUANTISE_H_LAG = 5
 SECOND_MATMUL_LAG = 6
+STORE_BUFFERS = 24
 
 VECTOR_OUT_SHARE = 4
 
@@ -49,7 +50,7 @@ def tile_multiscaleretention_pb_t_kernel(tc, x, y_norm, wg_w, wo_w, out):
         const = ctx.enter_context(tc.tile_pool(name="const", bufs=1))
         loads = ctx.enter_context(tc.tile_pool(name="loads", bufs=LOADS_AHEAD + 1))
         work = ctx.enter_context(tc.tile_pool(name="work", bufs=4))
-        stores = ctx.enter_context(tc.tile_pool(name="stores", bufs=10))
+        stores = ctx.enter_context(tc.tile_pool(name="stores", bufs=STORE_BUFFERS))
         psum_t = ctx.enter_context(tc.psum_pool(name="psum_t", bufs=1))
         psum_mx = ctx.enter_context(tc.psum_pool(name="psum_mx", bufs=3))
 
@@ -109,13 +110,12 @@ def tile_multiscaleretention_pb_t_kernel(tc, x, y_norm, wg_w, wo_w, out):
             )
             wo_mx["codes"], wo_mx["scales"] = quantise_weight(wo_grouped, "wo")
 
-        x_grouped = {}
         x_mx = {}
         g_banks = {}
         h_rows = {}
-        h_grouped = {}
         h_mx = {}
         out_banks = {}
+        grouped_steps = {}
 
         def transpose_x_round(r):
             c, first_sub = r // CHUNK_ROUNDS, (r % CHUNK_ROUNDS) * ROUND_SUBS
@@ -138,19 +138,29 @@ def tile_multiscaleretention_pb_t_kernel(tc, x, y_norm, wg_w, wo_w, out):
                     nc.tensor.transpose(bank[:, s, u, :], words[:, start : start + P], ident[:])
             return bank
 
-        def group_round(bank, tag):
-            tile_bf16 = work.tile([P, ROUND_COLS], BF16, tag=tag, align_bytes=64)
+        def group_round(bank, grouped, half):
+            words = grouped[:, half * ROUND_COLS : (half + 1) * ROUND_COLS].bitcast(F32)
             nc.scalar.copy(
-                out=tile_bf16[:].bitcast(F32).rearrange("p (s r u) -> p s r u", s=ROUND_SUBS, u=2),
+                out=words.rearrange("p (s r u) -> p s r u", s=ROUND_SUBS, u=2),
                 in_=bank[:].rearrange("p s u r -> p s r u"),
             )
-            return tile_bf16
 
-        def quantise_round(grouped, name):
-            codes = work.tile([P, ROUND_SUBS * P], U32, tag=name + "_codes", align_bytes=64)
-            scales = work.tile([P, ROUND_SUBS * P], U8, tag=name + "_scales", align_bytes=64)
-            nc.vector.quantize_mx(out=codes[:].bitcast(FP8X4), scales=scales[:], in_=grouped[:])
-            return codes, scales
+        def quantise_step(i):
+            halves = [("x", i), ("h", i - TRANSPOSE_H_LAG)]
+            there = [half for half in range(2) if 0 <= halves[half][1] < ROUNDS]
+            words = slice(there[0] * ROUND_WORDS, (there[-1] + 1) * ROUND_WORDS)
+            values = slice(there[0] * ROUND_COLS, (there[-1] + 1) * ROUND_COLS)
+            codes = work.tile([P, 2 * ROUND_WORDS], U32, tag="codes", align_bytes=64)
+            scales = work.tile([P, 2 * ROUND_WORDS], U8, tag="scales", align_bytes=64)
+            nc.vector.quantize_mx(
+                out=codes[:, words].bitcast(FP8X4),
+                scales=scales[:, words],
+                in_=grouped_steps[i][:, values],
+            )
+            for half in there:
+                operand, r = halves[half]
+                of_round = slice(half * ROUND_WORDS, (half + 1) * ROUND_WORDS)
+                (x_mx if operand == "x" else h_mx)[r] = (codes[:, of_round], scales[:, of_round])
 
         def first_matmul_round(r):
             codes, scales = x_mx[r]
@@ -221,29 +231,28 @@ def tile_multiscaleretention_pb_t_kernel(tc, x, y_norm, wg_w, wo_w, out):
         for i in range(ROUNDS + SECOND_MATMUL_LAG):
             if i % CHUNK_ROUNDS == 0 and i // CHUNK_ROUNDS + LOADS_AHEAD < CHUNKS:
                 load_chunk(i // CHUNK_ROUNDS + LOADS_AHEAD)
-            quantise_x_r = i - QUANTISE_X_LAG
             first_r = i - FIRST_MATMUL_LAG
             h_r = i - TRANSPOSE_H_LAG
-            quantise_h_r = i - QUANTISE_H_LAG
             second_r = i - SECOND_MATMUL_LAG
-            if 0 <= quantise_x_r < ROUNDS:
-                x_mx[quantise_x_r] = quantise_round(x_grouped[quantise_x_r], "x")
+            if i - QUANTISE_LAG in grouped_steps:
+                quantise_step(i - QUANTISE_LAG)
             if i == FIRST_MATMUL_LAG:
                 prepare_wo()
-            if 0 <= quantise_h_r < ROUNDS:
-                h_mx[quantise_h_r] = quantise_round(h_grouped[quantise_h_r], "h")
             if i < ROUNDS:
                 x_bank = transpose_x_round(i)
             if 0 <= h_r < ROUNDS:
                 h_bank = transpose_h_round(h_r)
+            if h_r < ROUNDS:
+                grouped = work.tile([P, 2 * ROUND_COLS], BF16, tag="grouped", align_bytes=64)
+                grouped_steps[i] = grouped
             if i < ROUNDS:
-                x_grouped[i] = group_round(x_bank, "x_grouped")
+                group_round(x_bank, grouped, 0)
             if 0 <= h_r < ROUNDS:
-                h_grouped[h_r] = group_round(h_bank, "h_grouped")
-            if 0 <= first_r < ROUNDS:
-                first_matmul_round(first_r)
+                group_round(h_bank, grouped, 1)
             if 0 <= second_r < ROUNDS:
                 second_matmul_round(second_r)
+            if 0 <= first_r < ROUNDS:
+                first_matmul_round(first_r)
             if 0 <= first_r < ROUNDS:
                 gate_round(first_r)
             if 0 <= second_r < ROUNDS:

@@ -29,6 +29,9 @@ QUANTISE_LAG = 1
 FIRST_MATMUL_LAG = 2
 TRANSPOSE_H_LAG = 4
 SECOND_MATMUL_LAG = 6
+EARLY_ROUNDS = FIRST_MATMUL_LAG + 1
+WARM_UP = 6
+VECTOR_WG_WORDS = 32
 STORE_BUFFERS = 24
 
 VECTOR_OUT_SHARE = 4
@@ -57,10 +60,9 @@ def tile_multiscaleretention_pb_t_kernel(tc, x, y_norm, wg_w, wo_w, out):
         x_chunks = {}
         y_chunks = {}
 
-        def load_rounds(c, first_round, rounds):
+        def load_rounds(chunks, rows, c, first_round, rounds):
             cols = slice(first_round * ROUND_COLS, (first_round + rounds) * ROUND_COLS)
-            nc.sync.dma_start(out=x_chunks[c][:, cols], in_=chunk_view(x_rows, c)[:, cols])
-            nc.sync.dma_start(out=y_chunks[c][:, cols], in_=chunk_view(y_rows, c)[:, cols])
+            nc.sync.dma_start(out=chunks[c][:, cols], in_=chunk_view(rows, c)[:, cols])
 
         def load_weight(w, name):
             raw = const.tile([P, PACK, D], BF16, name=name)
@@ -69,23 +71,42 @@ def tile_multiscaleretention_pb_t_kernel(tc, x, y_norm, wg_w, wo_w, out):
 
         weights_raw = {}
 
-        def load_chunk(c):
+        def make_chunk(c):
             x_sb = loads.tile([P, SUBS * D], BF16, tag="x")
             y_sb = loads.tile([P, SUBS * D], BF16, tag="y")
             x_chunks[c] = x_sb
             y_chunks[c] = y_sb
-            rounds = min(CHUNK_ROUNDS, 2**c)
-            for first_round in range(0, CHUNK_ROUNDS, rounds):
-                load_rounds(c, first_round, rounds)
-                if c == 0 and first_round == 0:
-                    weights_raw["wo"] = load_weight(wo_w, "wo_raw")
 
+        def load_chunk(c):
+            make_chunk(c)
+            load_rounds(x_chunks, x_rows, c, 0, CHUNK_ROUNDS)
+            load_rounds(y_chunks, y_rows, c, 0, CHUNK_ROUNDS)
+
+        make_chunk(0)
+        make_chunk(1)
+        load_rounds(x_chunks, x_rows, 0, 0, 1)
         weights_raw["wg"] = load_weight(wg_w, "wg_raw")
-        for c in range(LOADS_AHEAD):
+        load_rounds(x_chunks, x_rows, 0, 1, 1)
+        load_rounds(x_chunks, x_rows, 0, 2, 2)
+        load_rounds(y_chunks, y_rows, 0, 0, 1)
+        load_rounds(x_chunks, x_rows, 1, 0, 2)
+        load_rounds(y_chunks, y_rows, 0, 1, 1)
+        weights_raw["wo"] = load_weight(wo_w, "wo_raw")
+        load_rounds(y_chunks, y_rows, 0, 2, 2)
+        load_rounds(x_chunks, x_rows, 1, 2, 2)
+        load_rounds(y_chunks, y_rows, 1, 0, CHUNK_ROUNDS)
+        for c in range(2, LOADS_AHEAD):
             load_chunk(c)
 
+        zeros = const.tile([P, D], BF16)
+        nc.gpsimd.memset(zeros[:], 0.0)
         ident = const.tile([P, P], F32)
         make_identity(nc, ident[:])
+
+        def warm_up(count):
+            bank = psum_mx.tile([P, D], F32, tag="out")
+            for _ in range(count):
+                nc.tensor.matmul(bank[:], lhsT=zeros[:, :P], rhs=zeros[:], start=True, stop=True)
 
         def quantise_weight(grouped, name):
             codes = const.tile([P, D], U32, name=name + "_codes", align_bytes=64)
@@ -96,18 +117,25 @@ def tile_multiscaleretention_pb_t_kernel(tc, x, y_norm, wg_w, wo_w, out):
         wg_grouped = const.tile([P, D * PACK], BF16, align_bytes=64)
         wg_sorted = wg_grouped[:].rearrange("p (u q e t) -> p u q e t", u=2, e=2, t=PACK)
         wg_cols = weights_raw["wg"][:].rearrange("p t (q u e) -> p u q e t", u=2, e=2)
-        for u in range(2):
-            nc.vector.tensor_copy(out=wg_sorted[:, u], in_=wg_cols[:, u])
+        nc.vector.tensor_copy(out=wg_sorted[:, 0], in_=wg_cols[:, 0])
+        nc.vector.tensor_copy(out=wg_sorted[:, 1, :VECTOR_WG_WORDS], in_=wg_cols[:, 1, :VECTOR_WG_WORDS])
+        nc.scalar.copy(out=wg_sorted[:, 1, VECTOR_WG_WORDS:], in_=wg_cols[:, 1, VECTOR_WG_WORDS:])
         wg_codes, wg_scales = quantise_weight(wg_grouped, "wg")
 
         wo_mx = {}
+        wo_grouped = const.tile([P, D * PACK], BF16, align_bytes=64)
+        for piece in range(PACK):
+            cols = slice(piece * P, (piece + 1) * P)
+            nc.gpsimd.tensor_scalar(
+                out=wo_grouped[:].rearrange("p (c t) -> p c t", t=PACK)[:, cols],
+                in0=weights_raw["wo"][:].rearrange("p t c -> p c t")[:, cols],
+                scalar1=1.0,
+                scalar2=0.0,
+                op0=mybir.AluOpType.mult,
+                op1=mybir.AluOpType.add,
+            )
 
         def prepare_wo():
-            wo_grouped = const.tile([P, D * PACK], BF16, align_bytes=64)
-            nc.vector.tensor_copy(
-                out=wo_grouped[:].rearrange("p (c t) -> p c t", t=PACK),
-                in_=weights_raw["wo"][:].rearrange("p t c -> p c t"),
-            )
             wo_mx["codes"], wo_mx["scales"] = quantise_weight(wo_grouped, "wo")
 
         x_mx = {}
@@ -120,7 +148,10 @@ def tile_multiscaleretention_pb_t_kernel(tc, x, y_norm, wg_w, wo_w, out):
         def transpose_x_round(r):
             c, first_sub = r // CHUNK_ROUNDS, (r % CHUNK_ROUNDS) * ROUND_SUBS
             words = x_chunks[c][:].bitcast(F32)
-            bank = psum_t.tile([P, ROUND_SUBS, 2, P], F32, tag="xT")
+            if 0 < r < EARLY_ROUNDS:
+                bank = psum_mx.tile([P, ROUND_SUBS, 2, P], F32, tag="out")
+            else:
+                bank = psum_t.tile([P, ROUND_SUBS, 2, P], F32, tag="xT")
             for s in range(ROUND_SUBS):
                 for u in range(2):
                     start = (first_sub + s) * WORDS
@@ -236,10 +267,14 @@ def tile_multiscaleretention_pb_t_kernel(tc, x, y_norm, wg_w, wo_w, out):
             second_r = i - SECOND_MATMUL_LAG
             if i - QUANTISE_LAG in grouped_steps:
                 quantise_step(i - QUANTISE_LAG)
-            if i == FIRST_MATMUL_LAG:
+            if i == SECOND_MATMUL_LAG - 1:
                 prepare_wo()
+            if i == 0:
+                warm_up(WARM_UP)
             if i < ROUNDS:
                 x_bank = transpose_x_round(i)
+            if i < EARLY_ROUNDS - 1:
+                warm_up(1)
             if 0 <= h_r < ROUNDS:
                 h_bank = transpose_h_round(h_r)
             if h_r < ROUNDS:

@@ -31,6 +31,7 @@ TRANSPOSE_H_LAG = 4
 SECOND_MATMUL_LAG = 6
 EARLY_ROUNDS = FIRST_MATMUL_LAG + 1
 WARM_UP = 6
+BRIDGE = 64
 VECTOR_WG_WORDS = 32
 STORE_BUFFERS = 24
 
@@ -152,6 +153,8 @@ def tile_multiscaleretention_pb_t_kernel(tc, x, y_norm, wg_w, wo_w, out):
                 bank = psum_mx.tile([P, ROUND_SUBS, 2, P], F32, tag="out")
             else:
                 bank = psum_t.tile([P, ROUND_SUBS, 2, P], F32, tag="xT")
+            if FIRST_MATMUL_LAG < r < TRANSPOSE_H_LAG:
+                bridge(bank)
             for s in range(ROUND_SUBS):
                 for u in range(2):
                     start = (first_sub + s) * WORDS
@@ -163,11 +166,16 @@ def tile_multiscaleretention_pb_t_kernel(tc, x, y_norm, wg_w, wo_w, out):
         def transpose_h_round(r):
             words = h_rows[r][:].bitcast(F32)
             bank = psum_t.tile([P, ROUND_SUBS, 2, P], F32, tag="hT")
+            bridge(bank)
             for s in range(ROUND_SUBS):
                 for u in range(2):
                     start = (u * ROUND_SUBS + s) * P
                     nc.tensor.transpose(bank[:, s, u, :], words[:, start : start + P], ident[:])
             return bank
+
+        def bridge(bank):
+            flat = bank[:].rearrange("p a b c -> p (a b c)") if len(bank.shape) == 4 else bank[:]
+            nc.tensor.matmul(flat[:, :BRIDGE], lhsT=zeros[:, :P], rhs=zeros[:, :BRIDGE], start=True, stop=True)
 
         def group_round(bank, grouped, half):
             words = grouped[:, half * ROUND_COLS : (half + 1) * ROUND_COLS].bitcast(F32)
@@ -218,6 +226,8 @@ def tile_multiscaleretention_pb_t_kernel(tc, x, y_norm, wg_w, wo_w, out):
             for s in range(ROUND_SUBS):
                 tokens = slice(s * P, (s + 1) * P)
                 bank = psum_mx.tile([P, D], F32, tag="out")
+                if s == 0:
+                    bridge(bank)
                 nc.tensor.matmul_mx(
                     out=bank[:],
                     lhsT=codes[:, tokens].bitcast(FP8X4),
@@ -271,19 +281,19 @@ def tile_multiscaleretention_pb_t_kernel(tc, x, y_norm, wg_w, wo_w, out):
                 prepare_wo()
             if i == 0:
                 warm_up(WARM_UP)
+            if 0 <= h_r < ROUNDS:
+                h_bank = transpose_h_round(h_r)
             if i < ROUNDS:
                 x_bank = transpose_x_round(i)
             if i < EARLY_ROUNDS - 1:
                 warm_up(1)
-            if 0 <= h_r < ROUNDS:
-                h_bank = transpose_h_round(h_r)
             if h_r < ROUNDS:
                 grouped = work.tile([P, 2 * ROUND_COLS], BF16, tag="grouped", align_bytes=64)
                 grouped_steps[i] = grouped
-            if i < ROUNDS:
-                group_round(x_bank, grouped, 0)
             if 0 <= h_r < ROUNDS:
                 group_round(h_bank, grouped, 1)
+            if i < ROUNDS:
+                group_round(x_bank, grouped, 0)
             if 0 <= second_r < ROUNDS:
                 second_matmul_round(second_r)
             if 0 <= first_r < ROUNDS:

@@ -21,7 +21,8 @@ CHUNKS = TOKENS // CHUNK
 ROUND_SUBS = 2
 ROUND_COLS = ROUND_SUBS * D
 ROUND_WORDS = ROUND_SUBS * P
-ROUNDS = TOKENS // (ROUND_SUBS * P)
+ROUND_SIZES = [ROUND_SUBS] * (TOKENS // (ROUND_SUBS * P) - 1) + [1] * ROUND_SUBS
+ROUNDS = len(ROUND_SIZES)
 CHUNK_ROUNDS = SUBS // ROUND_SUBS
 LOADS_AHEAD = 3
 
@@ -30,12 +31,12 @@ FIRST_MATMUL_LAG = 2
 TRANSPOSE_H_LAG = 4
 SECOND_MATMUL_LAG = 6
 EARLY_ROUNDS = FIRST_MATMUL_LAG + 1
-WARM_UP = 6
+WARM_UP = 4
 BRIDGE = 64
-VECTOR_WG_WORDS = 32
+VECTOR_WG_WORDS = 80
 STORE_BUFFERS = 24
 
-VECTOR_OUT_SHARE = 4
+VECTOR_OUT_SHARE = 6
 
 FLOPS = 2 * 2 * TOKENS * D * D
 
@@ -118,10 +119,14 @@ def tile_multiscaleretention_pb_t_kernel(tc, x, y_norm, wg_w, wo_w, out):
         wg_grouped = const.tile([P, D * PACK], BF16, align_bytes=64)
         wg_sorted = wg_grouped[:].rearrange("p (u q e t) -> p u q e t", u=2, e=2, t=PACK)
         wg_cols = weights_raw["wg"][:].rearrange("p t (q u e) -> p u q e t", u=2, e=2)
-        nc.vector.tensor_copy(out=wg_sorted[:, 0], in_=wg_cols[:, 0])
-        nc.vector.tensor_copy(out=wg_sorted[:, 1, :VECTOR_WG_WORDS], in_=wg_cols[:, 1, :VECTOR_WG_WORDS])
-        nc.scalar.copy(out=wg_sorted[:, 1, VECTOR_WG_WORDS:], in_=wg_cols[:, 1, VECTOR_WG_WORDS:])
-        wg_codes, wg_scales = quantise_weight(wg_grouped, "wg")
+        wg_mx = {}
+
+        def prepare_wg():
+            mine, others = slice(0, VECTOR_WG_WORDS), slice(VECTOR_WG_WORDS, P)
+            nc.vector.tensor_copy(out=wg_sorted[:, 0], in_=wg_cols[:, 0])
+            nc.vector.tensor_copy(out=wg_sorted[:, 1, mine], in_=wg_cols[:, 1, mine])
+            nc.scalar.copy(out=wg_sorted[:, 1, others], in_=wg_cols[:, 1, others])
+            wg_mx["codes"], wg_mx["scales"] = quantise_weight(wg_grouped, "wg")
 
         wo_mx = {}
         wo_grouped = const.tile([P, D * PACK], BF16, align_bytes=64)
@@ -140,14 +145,18 @@ def tile_multiscaleretention_pb_t_kernel(tc, x, y_norm, wg_w, wo_w, out):
             wo_mx["codes"], wo_mx["scales"] = quantise_weight(wo_grouped, "wo")
 
         x_mx = {}
-        g_banks = {}
+        g_halves = {}
         h_rows = {}
         h_mx = {}
         out_banks = {}
         grouped_steps = {}
 
+        def place(r):
+            first_sub = sum(ROUND_SIZES[:r])
+            return first_sub // SUBS, first_sub % SUBS, ROUND_SIZES[r]
+
         def transpose_x_round(r):
-            c, first_sub = r // CHUNK_ROUNDS, (r % CHUNK_ROUNDS) * ROUND_SUBS
+            c, first_sub, subs = place(r)
             words = x_chunks[c][:].bitcast(F32)
             if 0 < r < EARLY_ROUNDS:
                 bank = psum_mx.tile([P, ROUND_SUBS, 2, P], F32, tag="out")
@@ -155,7 +164,7 @@ def tile_multiscaleretention_pb_t_kernel(tc, x, y_norm, wg_w, wo_w, out):
                 bank = psum_t.tile([P, ROUND_SUBS, 2, P], F32, tag="xT")
             if FIRST_MATMUL_LAG < r < TRANSPOSE_H_LAG:
                 bridge(bank)
-            for s in range(ROUND_SUBS):
+            for s in range(subs):
                 for u in range(2):
                     start = (first_sub + s) * WORDS
                     nc.tensor.transpose(
@@ -167,9 +176,10 @@ def tile_multiscaleretention_pb_t_kernel(tc, x, y_norm, wg_w, wo_w, out):
             words = h_rows[r][:].bitcast(F32)
             bank = psum_t.tile([P, ROUND_SUBS, 2, P], F32, tag="hT")
             bridge(bank)
-            for s in range(ROUND_SUBS):
+            subs = ROUND_SIZES[r]
+            for s in range(subs):
                 for u in range(2):
-                    start = (u * ROUND_SUBS + s) * P
+                    start = (u * subs + s) * P
                     nc.tensor.transpose(bank[:, s, u, :], words[:, start : start + P], ident[:])
             return bank
 
@@ -177,53 +187,60 @@ def tile_multiscaleretention_pb_t_kernel(tc, x, y_norm, wg_w, wo_w, out):
             flat = bank[:].rearrange("p a b c -> p (a b c)") if len(bank.shape) == 4 else bank[:]
             nc.tensor.matmul(flat[:, :BRIDGE], lhsT=zeros[:, :P], rhs=zeros[:, :BRIDGE], start=True, stop=True)
 
-        def group_round(bank, grouped, half):
-            words = grouped[:, half * ROUND_COLS : (half + 1) * ROUND_COLS].bitcast(F32)
+        def group_round(r, bank, grouped, half):
+            subs = ROUND_SIZES[r]
+            words = grouped[:, half * ROUND_COLS : half * ROUND_COLS + subs * D].bitcast(F32)
             nc.scalar.copy(
-                out=words.rearrange("p (s r u) -> p s r u", s=ROUND_SUBS, u=2),
-                in_=bank[:].rearrange("p s u r -> p s r u"),
+                out=words.rearrange("p (s r u) -> p s r u", s=subs, u=2),
+                in_=bank[:, :subs].rearrange("p s u r -> p s r u"),
             )
 
         def quantise_step(i):
-            halves = [("x", i), ("h", i - TRANSPOSE_H_LAG)]
-            there = [half for half in range(2) if 0 <= halves[half][1] < ROUNDS]
-            words = slice(there[0] * ROUND_WORDS, (there[-1] + 1) * ROUND_WORDS)
-            values = slice(there[0] * ROUND_COLS, (there[-1] + 1) * ROUND_COLS)
             codes = work.tile([P, 2 * ROUND_WORDS], U32, tag="codes", align_bytes=64)
             scales = work.tile([P, 2 * ROUND_WORDS], U8, tag="scales", align_bytes=64)
-            nc.vector.quantize_mx(
-                out=codes[:, words].bitcast(FP8X4),
-                scales=scales[:, words],
-                in_=grouped_steps[i][:, values],
-            )
-            for half in there:
-                operand, r = halves[half]
-                of_round = slice(half * ROUND_WORDS, (half + 1) * ROUND_WORDS)
-                (x_mx if operand == "x" else h_mx)[r] = (codes[:, of_round], scales[:, of_round])
+            spans = {}
+            for half, r in ((0, i), (1, i - TRANSPOSE_H_LAG)):
+                if 0 <= r < ROUNDS:
+                    start = half * ROUND_WORDS
+                    spans[half] = slice(start, start + ROUND_SIZES[r] * P)
+                    (h_mx if half else x_mx)[r] = (codes[:, spans[half]], scales[:, spans[half]])
+            if len(spans) == 2 and spans[0].stop == spans[1].start and spans[1].stop == 2 * ROUND_WORDS:
+                runs = [slice(0, 2 * ROUND_WORDS)]
+            else:
+                runs = list(spans.values())
+            for run in runs:
+                nc.vector.quantize_mx(
+                    out=codes[:, run].bitcast(FP8X4),
+                    scales=scales[:, run],
+                    in_=grouped_steps[i][:, run.start * PACK : run.stop * PACK],
+                )
 
         def first_matmul_round(r):
             codes, scales = x_mx[r]
-            g_banks[r] = []
+            subs = ROUND_SIZES[r]
+            g_halves[r] = []
             for u in range(2):
                 cols = slice(u * WORDS, (u + 1) * WORDS)
-                bank = psum_mx.tile([P, ROUND_SUBS, WORDS], F32, tag="g")
-                for s in range(ROUND_SUBS):
+                if u * subs % ROUND_SUBS == 0:
+                    bank = psum_mx.tile([P, ROUND_SUBS, WORDS], F32, tag="g")
+                first = u * subs % ROUND_SUBS
+                for s in range(subs):
                     tokens = slice(s * P, (s + 1) * P)
                     nc.tensor.matmul_mx(
-                        out=bank[:, s, :],
+                        out=bank[:, first + s, :],
                         lhsT=codes[:, tokens].bitcast(FP8X4),
                         lhsT_scale=scales[:, tokens],
-                        rhs=wg_codes[:, cols].bitcast(FP8X4),
-                        rhs_scale=wg_scales[:, cols],
+                        rhs=wg_mx["codes"][:, cols].bitcast(FP8X4),
+                        rhs_scale=wg_mx["scales"][:, cols],
                         start=True,
                         stop=True,
                     )
-                g_banks[r].append(bank)
+                g_halves[r].append(bank[:, first : first + subs])
 
         def second_matmul_round(r):
             codes, scales = h_mx[r]
             out_banks[r] = []
-            for s in range(ROUND_SUBS):
+            for s in range(ROUND_SIZES[r]):
                 tokens = slice(s * P, (s + 1) * P)
                 bank = psum_mx.tile([P, D], F32, tag="out")
                 if s == 0:
@@ -240,14 +257,15 @@ def tile_multiscaleretention_pb_t_kernel(tc, x, y_norm, wg_w, wo_w, out):
                 out_banks[r].append(bank)
 
         def gate_round(r):
-            c, first = r // CHUNK_ROUNDS, (r % CHUNK_ROUNDS) * ROUND_COLS
-            y_words = y_chunks[c][:, first : first + ROUND_COLS].rearrange("p (q u e) -> p u q e", u=2, e=2)
-            h_bf16 = work.tile([P, ROUND_COLS], BF16, tag="h_rows", align_bytes=64)
+            c, first_sub, subs = place(r)
+            y_round = y_chunks[c][:, first_sub * D : (first_sub + subs) * D]
+            y_words = y_round.rearrange("p (q u e) -> p u q e", u=2, e=2)
+            h_bf16 = work.tile([P, subs * D], BF16, tag="h_rows", align_bytes=64)
             h_words = h_bf16[:].rearrange("p (u q e) -> p u q e", u=2, e=2)
             for u in range(2):
                 nc.vector.scalar_tensor_tensor(
                     out=h_words[:, u],
-                    in0=g_banks[r][u][:].rearrange("p s (q e) -> p (s q) e", e=2),
+                    in0=g_halves[r][u].rearrange("p s (q e) -> p (s q) e", e=2),
                     scalar=0.0,
                     in1=y_words[:, u],
                     op0=mybir.AluOpType.max,
@@ -256,17 +274,18 @@ def tile_multiscaleretention_pb_t_kernel(tc, x, y_norm, wg_w, wo_w, out):
             h_rows[r] = h_bf16
 
         def store_round(r):
-            out_sb = stores.tile([P, ROUND_COLS], F32)
-            for s in range(ROUND_SUBS):
+            c, first_sub, subs = place(r)
+            out_sb = stores.tile([P, subs * D], F32)
+            for s in range(subs):
                 span = slice(s * D, (s + 1) * D)
-                if (r * ROUND_SUBS + s) % VECTOR_OUT_SHARE == VECTOR_OUT_SHARE - 1:
+                sub = c * SUBS + first_sub + s
+                idle = r + SECOND_MATMUL_LAG >= ROUNDS + FIRST_MATMUL_LAG
+                if sub % VECTOR_OUT_SHARE == VECTOR_OUT_SHARE - 1 or (idle and sub % 2 == 1):
                     nc.vector.tensor_copy(out=out_sb[:, span], in_=out_banks[r][s][:])
                 else:
                     nc.scalar.copy(out=out_sb[:, span], in_=out_banks[r][s][:])
-            first = (r % CHUNK_ROUNDS) * ROUND_COLS
             nc.sync.dma_start(
-                out=chunk_view(out_rows, r // CHUNK_ROUNDS)[:, first : first + ROUND_COLS],
-                in_=out_sb[:],
+                out=chunk_view(out_rows, c)[:, first_sub * D : (first_sub + subs) * D], in_=out_sb[:]
             )
 
         for i in range(ROUNDS + SECOND_MATMUL_LAG):
@@ -285,15 +304,17 @@ def tile_multiscaleretention_pb_t_kernel(tc, x, y_norm, wg_w, wo_w, out):
                 h_bank = transpose_h_round(h_r)
             if i < ROUNDS:
                 x_bank = transpose_x_round(i)
-            if i < EARLY_ROUNDS - 1:
+            if i < SECOND_MATMUL_LAG:
                 warm_up(1)
             if h_r < ROUNDS:
                 grouped = work.tile([P, 2 * ROUND_COLS], BF16, tag="grouped", align_bytes=64)
                 grouped_steps[i] = grouped
             if 0 <= h_r < ROUNDS:
-                group_round(h_bank, grouped, 1)
+                group_round(h_r, h_bank, grouped, 1)
             if i < ROUNDS:
-                group_round(x_bank, grouped, 0)
+                group_round(i, x_bank, grouped, 0)
+            if i == 0:
+                prepare_wg()
             if 0 <= second_r < ROUNDS:
                 second_matmul_round(second_r)
             if 0 <= first_r < ROUNDS:

@@ -56,8 +56,7 @@ def tile_multiscaleretention_pb_t_kernel(tc, x, y_norm, wg_w, wo_w, out):
         loads = ctx.enter_context(tc.tile_pool(name="loads", bufs=LOADS_AHEAD + 1))
         work = ctx.enter_context(tc.tile_pool(name="work", bufs=4))
         stores = ctx.enter_context(tc.tile_pool(name="stores", bufs=STORE_BUFFERS))
-        psum_t = ctx.enter_context(tc.psum_pool(name="psum_t", bufs=1))
-        psum_mx = ctx.enter_context(tc.psum_pool(name="psum_mx", bufs=3))
+        psum = ctx.enter_context(tc.psum_pool(name="psum", bufs=8))
 
         x_chunks = {}
         y_chunks = {}
@@ -106,7 +105,7 @@ def tile_multiscaleretention_pb_t_kernel(tc, x, y_norm, wg_w, wo_w, out):
         make_identity(nc, ident[:])
 
         def warm_up(count):
-            bank = psum_mx.tile([P, D], F32, tag="out")
+            bank = psum.tile([P, D], F32, tag="bank")
             for _ in range(count):
                 nc.tensor.matmul(bank[:], lhsT=zeros[:, :P], rhs=zeros[:], start=True, stop=True)
 
@@ -158,10 +157,7 @@ def tile_multiscaleretention_pb_t_kernel(tc, x, y_norm, wg_w, wo_w, out):
         def transpose_x_round(r):
             c, first_sub, subs = place(r)
             words = x_chunks[c][:].bitcast(F32)
-            if 0 < r < EARLY_ROUNDS:
-                bank = psum_mx.tile([P, ROUND_SUBS, 2, P], F32, tag="out")
-            else:
-                bank = psum_t.tile([P, ROUND_SUBS, 2, P], F32, tag="xT")
+            bank = psum.tile([P, ROUND_SUBS, 2, P], F32, tag="bank")
             if FIRST_MATMUL_LAG < r < TRANSPOSE_H_LAG:
                 bridge(bank)
             for s in range(subs):
@@ -174,7 +170,7 @@ def tile_multiscaleretention_pb_t_kernel(tc, x, y_norm, wg_w, wo_w, out):
 
         def transpose_h_round(r):
             words = h_rows[r][:].bitcast(F32)
-            bank = psum_t.tile([P, ROUND_SUBS, 2, P], F32, tag="hT")
+            bank = psum.tile([P, ROUND_SUBS, 2, P], F32, tag="bank")
             bridge(bank)
             subs = ROUND_SIZES[r]
             for s in range(subs):
@@ -222,7 +218,7 @@ def tile_multiscaleretention_pb_t_kernel(tc, x, y_norm, wg_w, wo_w, out):
             for u in range(2):
                 cols = slice(u * WORDS, (u + 1) * WORDS)
                 if u * subs % ROUND_SUBS == 0:
-                    bank = psum_mx.tile([P, ROUND_SUBS, WORDS], F32, tag="g")
+                    bank = psum.tile([P, ROUND_SUBS, WORDS], F32, tag="bank")
                 first = u * subs % ROUND_SUBS
                 for s in range(subs):
                     tokens = slice(s * P, (s + 1) * P)
@@ -242,7 +238,7 @@ def tile_multiscaleretention_pb_t_kernel(tc, x, y_norm, wg_w, wo_w, out):
             out_banks[r] = []
             for s in range(ROUND_SIZES[r]):
                 tokens = slice(s * P, (s + 1) * P)
-                bank = psum_mx.tile([P, D], F32, tag="out")
+                bank = psum.tile([P, D], F32, tag="bank")
                 if s == 0:
                     bridge(bank)
                 nc.tensor.matmul_mx(
@@ -276,7 +272,7 @@ def tile_multiscaleretention_pb_t_kernel(tc, x, y_norm, wg_w, wo_w, out):
         def store_round(r):
             c, first_sub, subs = place(r)
             out_sb = stores.tile([P, subs * D], F32)
-            for s in range(subs):
+            for s in reversed(range(subs)):
                 span = slice(s * D, (s + 1) * D)
                 sub = c * SUBS + first_sub + s
                 idle = r + SECOND_MATMUL_LAG >= ROUNDS + FIRST_MATMUL_LAG
@@ -309,10 +305,10 @@ def tile_multiscaleretention_pb_t_kernel(tc, x, y_norm, wg_w, wo_w, out):
             if h_r < ROUNDS:
                 grouped = work.tile([P, 2 * ROUND_COLS], BF16, tag="grouped", align_bytes=64)
                 grouped_steps[i] = grouped
-            if 0 <= h_r < ROUNDS:
-                group_round(h_r, h_bank, grouped, 1)
             if i < ROUNDS:
                 group_round(i, x_bank, grouped, 0)
+            if 0 <= h_r < ROUNDS:
+                group_round(h_r, h_bank, grouped, 1)
             if i == 0:
                 prepare_wg()
             if 0 <= second_r < ROUNDS:

@@ -31,6 +31,8 @@ FIRST_MATMUL_LAG = 2
 TRANSPOSE_H_LAG = 4
 SECOND_MATMUL_LAG = 6
 EARLY_ROUNDS = FIRST_MATMUL_LAG + 1
+SORTED_SUB = 1
+FIRST_SORTED = 6
 WARM_UP = 4
 BRIDGE = 64
 VECTOR_WG_WORDS = 80
@@ -143,6 +145,7 @@ def tile_multiscaleretention_pb_t_kernel(tc, x, y_norm, wg_w, wo_w, out):
         def prepare_wo():
             wo_mx["codes"], wo_mx["scales"] = quantise_weight(wo_grouped, "wo")
 
+        x_sorted = {}
         x_mx = {}
         g_halves = {}
         h_rows = {}
@@ -154,6 +157,22 @@ def tile_multiscaleretention_pb_t_kernel(tc, x, y_norm, wg_w, wo_w, out):
             first_sub = sum(ROUND_SIZES[:r])
             return first_sub // SUBS, first_sub % SUBS, ROUND_SIZES[r]
 
+        def sort_x_round(r, tile_bf16):
+            c, first_sub, subs = place(r)
+            start = (first_sub + SORTED_SUB) * D
+            by_u = x_chunks[c][:, start : start + D].rearrange("p (q u e) -> p u q e", u=2, e=2)
+            out_by_u = tile_bf16.rearrange("p (u q e) -> p u q e", u=2, e=2)
+            for u in range(2):
+                nc.gpsimd.tensor_scalar(
+                    out=out_by_u[:, u],
+                    in0=by_u[:, u],
+                    scalar1=1.0,
+                    scalar2=0.0,
+                    op0=mybir.AluOpType.mult,
+                    op1=mybir.AluOpType.add,
+                )
+            x_sorted[r] = tile_bf16.bitcast(F32)
+
         def transpose_x_round(r):
             c, first_sub, subs = place(r)
             words = x_chunks[c][:].bitcast(F32)
@@ -163,9 +182,11 @@ def tile_multiscaleretention_pb_t_kernel(tc, x, y_norm, wg_w, wo_w, out):
             for s in range(subs):
                 for u in range(2):
                     start = (first_sub + s) * WORDS
-                    nc.tensor.transpose(
-                        bank[:, s, u, :], words[:, start + u : start + WORDS : 2], ident[:]
-                    )
+                    if s == SORTED_SUB and r in x_sorted:
+                        of_u = x_sorted[r][:, u * P : (u + 1) * P]
+                    else:
+                        of_u = words[:, start + u : start + WORDS : 2]
+                    nc.tensor.transpose(bank[:, s, u, :], of_u, ident[:])
             return bank
 
         def transpose_h_round(r):
@@ -303,8 +324,10 @@ def tile_multiscaleretention_pb_t_kernel(tc, x, y_norm, wg_w, wo_w, out):
             if i < SECOND_MATMUL_LAG:
                 warm_up(1)
             if h_r < ROUNDS:
-                grouped = work.tile([P, 2 * ROUND_COLS], BF16, tag="grouped", align_bytes=64)
+                grouped = work.tile([P, 2 * ROUND_COLS + D], BF16, tag="grouped", align_bytes=64)
                 grouped_steps[i] = grouped
+                if FIRST_SORTED <= i + 1 < ROUNDS and ROUND_SIZES[i + 1] > SORTED_SUB:
+                    sort_x_round(i + 1, grouped[:, 2 * ROUND_COLS :])
             if i < ROUNDS:
                 group_round(i, x_bank, grouped, 0)
             if 0 <= h_r < ROUNDS:

from contextlib import ExitStack

import concourse.mybir as mybir
from concourse.masks import make_identity

BF16 = mybir.dt.bfloat16
F32 = mybir.dt.float32
U32 = mybir.dt.uint32
U8 = mybir.dt.uint8
FP8X4 = mybir.dt.float8_e4m3fn_x4

P = 128
PACK = 4
D = P * PACK
WORDS = D // 2
TOKENS = 4 * 2048

SUBS = 8
CHUNK = SUBS * P
CHUNKS = TOKENS // CHUNK
ROUND_SUBS = 2
ROUND_COLS = ROUND_SUBS * D
ROUND_WORDS = ROUND_SUBS * P
ROUND_SIZES = [ROUND_SUBS] * (TOKENS // (ROUND_SUBS * P) - 1) + [1] * ROUND_SUBS
ROUNDS = len(ROUND_SIZES)
CHUNK_ROUNDS = SUBS // ROUND_SUBS
LOADS_AHEAD = 3

QUANTISE_LAG = 1
FIRST_MATMUL_LAG = 2
TRANSPOSE_H_LAG = 4
SECOND_MATMUL_LAG = 6
EARLY_ROUNDS = FIRST_MATMUL_LAG + 1
SORTED_SUB = 1
FIRST_SORTED = 6
WARM_UP = 4
BRIDGE = 64
VECTOR_WG_WORDS = 80
STORE_BUFFERS = 24

VECTOR_OUT_SHARE = 6

FLOPS = 2 * 2 * TOKENS * D * D


def tile_multiscaleretention_pb_t_kernel(tc, x, y_norm, wg_w, wo_w, out):
    nc = tc.nc
    x_rows = x.flatten_outer_dims()
    y_rows = y_norm.flatten_outer_dims()
    out_rows = out.flatten_outer_dims()

    def chunk_view(rows, c):
        return rows[c * CHUNK : (c + 1) * CHUNK, :].rearrange("(p s) d -> p (s d)", s=SUBS)

    with ExitStack() as ctx:
        ctx.enter_context(tc.manual_schedule())
        const = ctx.enter_context(tc.tile_pool(name="const", bufs=1))
        loads = ctx.enter_context(tc.tile_pool(name="loads", bufs=LOADS_AHEAD + 1))
        work = ctx.enter_context(tc.tile_pool(name="work", bufs=4))
        stores = ctx.enter_context(tc.tile_pool(name="stores", bufs=STORE_BUFFERS))
        psum = ctx.enter_context(tc.psum_pool(name="psum", bufs=8))

        x_chunks = {}
        y_chunks = {}

        def load_rounds(chunks, rows, c, first_round, rounds):
            cols = slice(first_round * ROUND_COLS, (first_round + rounds) * ROUND_COLS)
            nc.sync.dma_start(out=chunks[c][:, cols], in_=chunk_view(rows, c)[:, cols])

        def load_weight(w, name):
            raw = const.tile([P, PACK, D], BF16, name=name)
            nc.sync.dma_start(out=raw[:], in_=w.rearrange("(p t) c -> p t c", t=PACK))
            return raw

        weights_raw = {}

        def make_chunk(c):
            x_sb = loads.tile([P, SUBS * D], BF16, tag="x")
            y_sb = loads.tile([P, SUBS * D], BF16, tag="y")
            x_chunks[c] = x_sb
            y_chunks[c] = y_sb

        def load_chunk(c):
            make_chunk(c)
            load_rounds(x_chunks, x_rows, c, 0, CHUNK_ROUNDS)
            load_rounds(y_chunks, y_rows, c, 0, CHUNK_ROUNDS)

        make_chunk(0)
        make_chunk(1)
        load_rounds(x_chunks, x_rows, 0, 0, 1)
        weights_raw["wg"] = load_weight(wg_w, "wg_raw")
        load_rounds(x_chunks, x_rows, 0, 1, 1)
        load_rounds(x_chunks, x_rows, 0, 2, 2)
        load_rounds(y_chunks, y_rows, 0, 0, 1)
        load_rounds(x_chunks, x_rows, 1, 0, 2)
        load_rounds(y_chunks, y_rows, 0, 1, 1)
        weights_raw["wo"] = load_weight(wo_w, "wo_raw")
        load_rounds(y_chunks, y_rows, 0, 2, 2)
        load_rounds(x_chunks, x_rows, 1, 2, 2)
        load_rounds(y_chunks, y_rows, 1, 0, CHUNK_ROUNDS)
        for c in range(2, LOADS_AHEAD):
            load_chunk(c)

        zeros = const.tile([P, D], BF16)
        nc.gpsimd.memset(zeros[:], 0.0)
        ident = const.tile([P, P], F32)
        make_identity(nc, ident[:])

        def warm_up(count):
            bank = psum.tile([P, D], F32, tag="bank")
            for _ in range(count):
                nc.tensor.matmul(bank[:], lhsT=zeros[:, :P], rhs=zeros[:], start=True, stop=True)

        def quantise_weight(grouped, name):
            codes = const.tile([P, D], U32, name=name + "_codes", align_bytes=64)
            scales = const.tile([P, D], U8, name=name + "_scales", align_bytes=64)
            nc.vector.quantize_mx(out=codes[:].bitcast(FP8X4), scales=scales[:], in_=grouped[:])
            return codes, scales

        wg_grouped = const.tile([P, D * PACK], BF16, align_bytes=64)
        wg_sorted = wg_grouped[:].rearrange("p (u q e t) -> p u q e t", u=2, e=2, t=PACK)
        wg_cols = weights_raw["wg"][:].rearrange("p t (q u e) -> p u q e t", u=2, e=2)
        wg_mx = {}

        def prepare_wg():
            mine, others = slice(0, VECTOR_WG_WORDS), slice(VECTOR_WG_WORDS, P)
            nc.vector.tensor_copy(out=wg_sorted[:, 0], in_=wg_cols[:, 0])
            nc.vector.tensor_copy(out=wg_sorted[:, 1, mine], in_=wg_cols[:, 1, mine])
            nc.scalar.copy(out=wg_sorted[:, 1, others], in_=wg_cols[:, 1, others])
            wg_mx["codes"], wg_mx["scales"] = quantise_weight(wg_grouped, "wg")

        wo_mx = {}
        wo_grouped = const.tile([P, D * PACK], BF16, align_bytes=64)
        for piece in range(PACK):
            cols = slice(piece * P, (piece + 1) * P)
            nc.gpsimd.tensor_scalar(
                out=wo_grouped[:].rearrange("p (c t) -> p c t", t=PACK)[:, cols],
                in0=weights_raw["wo"][:].rearrange("p t c -> p c t")[:, cols],
                scalar1=1.0,
                scalar2=0.0,
                op0=mybir.AluOpType.mult,
                op1=mybir.AluOpType.add,
            )

        def prepare_wo():
            wo_mx["codes"], wo_mx["scales"] = quantise_weight(wo_grouped, "wo")

        x_sorted = {}
        x_mx = {}
        g_halves = {}
        h_rows = {}
        h_mx = {}
        out_banks = {}
        grouped_steps = {}

        def place(r):
            first_sub = sum(ROUND_SIZES[:r])
            return first_sub // SUBS, first_sub % SUBS, ROUND_SIZES[r]

        def sort_x_round(r, tile_bf16):
            c, first_sub, subs = place(r)
            start = (first_sub + SORTED_SUB) * D
            by_u = x_chunks[c][:, start : start + D].rearrange("p (q u e) -> p u q e", u=2, e=2)
            out_by_u = tile_bf16.rearrange("p (u q e) -> p u q e", u=2, e=2)
            for u in range(2):
                nc.gpsimd.tensor_scalar(
                    out=out_by_u[:, u],
                    in0=by_u[:, u],
                    scalar1=1.0,
                    scalar2=0.0,
                    op0=mybir.AluOpType.mult,
                    op1=mybir.AluOpType.add,
                )
            x_sorted[r] = tile_bf16.bitcast(F32)

        def transpose_x_round(r):
            c, first_sub, subs = place(r)
            words = x_chunks[c][:].bitcast(F32)
            bank = psum.tile([P, ROUND_SUBS, 2, P], F32, tag="bank")
            if FIRST_MATMUL_LAG < r < TRANSPOSE_H_LAG:
                bridge(bank)
            for s in range(subs):
                for u in range(2):
                    start = (first_sub + s) * WORDS
                    if s == SORTED_SUB and r in x_sorted:
                        of_u = x_sorted[r][:, u * P : (u + 1) * P]
                    else:
                        of_u = words[:, start + u : start + WORDS : 2]
                    nc.tensor.transpose(bank[:, s, u, :], of_u, ident[:])
            return bank

        def transpose_h_round(r):
            words = h_rows[r][:].bitcast(F32)
            bank = psum.tile([P, ROUND_SUBS, 2, P], F32, tag="bank")
            bridge(bank)
            subs = ROUND_SIZES[r]
            for s in range(subs):
                for u in range(2):
                    start = (u * subs + s) * P
                    nc.tensor.transpose(bank[:, s, u, :], words[:, start : start + P], ident[:])
            return bank

        def bridge(bank):
            flat = bank[:].rearrange("p a b c -> p (a b c)") if len(bank.shape) == 4 else bank[:]
            nc.tensor.matmul(flat[:, :BRIDGE], lhsT=zeros[:, :P], rhs=zeros[:, :BRIDGE], start=True, stop=True)

        def group_round(r, bank, grouped, half):
            subs = ROUND_SIZES[r]
            words = grouped[:, half * ROUND_COLS : half * ROUND_COLS + subs * D].bitcast(F32)
            nc.scalar.copy(
                out=words.rearrange("p (s r u) -> p s r u", s=subs, u=2),
                in_=bank[:, :subs].rearrange("p s u r -> p s r u"),
            )

        def quantise_step(i):
            codes = work.tile([P, 2 * ROUND_WORDS], U32, tag="codes", align_bytes=64)
            scales = work.tile([P, 2 * ROUND_WORDS], U8, tag="scales", align_bytes=64)
            spans = {}
            for half, r in ((0, i), (1, i - TRANSPOSE_H_LAG)):
                if 0 <= r < ROUNDS:
                    start = half * ROUND_WORDS
                    spans[half] = slice(start, start + ROUND_SIZES[r] * P)
                    (h_mx if half else x_mx)[r] = (codes[:, spans[half]], scales[:, spans[half]])
            if len(spans) == 2 and spans[0].stop == spans[1].start and spans[1].stop == 2 * ROUND_WORDS:
                runs = [slice(0, 2 * ROUND_WORDS)]
            else:
                runs = list(spans.values())
            for run in runs:
                nc.vector.quantize_mx(
                    out=codes[:, run].bitcast(FP8X4),
                    scales=scales[:, run],
                    in_=grouped_steps[i][:, run.start * PACK : run.stop * PACK],
                )

        def first_matmul_round(r):
            codes, scales = x_mx[r]
            subs = ROUND_SIZES[r]
            g_halves[r] = []
            for u in range(2):
                cols = slice(u * WORDS, (u + 1) * WORDS)
                if u * subs % ROUND_SUBS == 0:
                    bank = psum.tile([P, ROUND_SUBS, WORDS], F32, tag="bank")
                first = u * subs % ROUND_SUBS
                for s in range(subs):
                    tokens = slice(s * P, (s + 1) * P)
                    nc.tensor.matmul_mx(
                        out=bank[:, first + s, :],
                        lhsT=codes[:, tokens].bitcast(FP8X4),
                        lhsT_scale=scales[:, tokens],
                        rhs=wg_mx["codes"][:, cols].bitcast(FP8X4),
                        rhs_scale=wg_mx["scales"][:, cols],
                        start=True,
                        stop=True,
                    )
                g_halves[r].append(bank[:, first : first + subs])

        def second_matmul_round(r):
            codes, scales = h_mx[r]
            out_banks[r] = []
            for s in range(ROUND_SIZES[r]):
                tokens = slice(s * P, (s + 1) * P)
                bank = psum.tile([P, D], F32, tag="bank")
                if s == 0:
                    bridge(bank)
                nc.tensor.matmul_mx(
                    out=bank[:],
                    lhsT=codes[:, tokens].bitcast(FP8X4),
                    lhsT_scale=scales[:, tokens],
                    rhs=wo_mx["codes"][:].bitcast(FP8X4),
                    rhs_scale=wo_mx["scales"][:],
                    start=True,
                    stop=True,
                )
                out_banks[r].append(bank)

        def gate_round(r):
            c, first_sub, subs = place(r)
            y_round = y_chunks[c][:, first_sub * D : (first_sub + subs) * D]
            y_words = y_round.rearrange("p (q u e) -> p u q e", u=2, e=2)
            h_bf16 = work.tile([P, subs * D], BF16, tag="h_rows", align_bytes=64)
            h_words = h_bf16[:].rearrange("p (u q e) -> p u q e", u=2, e=2)
            for u in range(2):
                nc.vector.scalar_tensor_tensor(
                    out=h_words[:, u],
                    in0=g_halves[r][u].rearrange("p s (q e) -> p (s q) e", e=2),
                    scalar=0.0,
                    in1=y_words[:, u],
                    op0=mybir.AluOpType.max,
                    op1=mybir.AluOpType.mult,
                )
            h_rows[r] = h_bf16

        def store_round(r):
            c, first_sub, subs = place(r)
            out_sb = stores.tile([P, subs * D], F32)
            for s in reversed(range(subs)):
                span = slice(s * D, (s + 1) * D)
                sub = c * SUBS + first_sub + s
                idle = r + SECOND_MATMUL_LAG >= ROUNDS + FIRST_MATMUL_LAG
                if sub % VECTOR_OUT_SHARE == VECTOR_OUT_SHARE - 1 or (idle and sub % 2 == 1):
                    nc.vector.tensor_copy(out=out_sb[:, span], in_=out_banks[r][s][:])
                else:
                    nc.scalar.copy(out=out_sb[:, span], in_=out_banks[r][s][:])
            nc.sync.dma_start(
                out=chunk_view(out_rows, c)[:, first_sub * D : (first_sub + subs) * D], in_=out_sb[:]
            )

        for i in range(ROUNDS + SECOND_MATMUL_LAG):
            if i % CHUNK_ROUNDS == 0 and i // CHUNK_ROUNDS + LOADS_AHEAD < CHUNKS:
                load_chunk(i // CHUNK_ROUNDS + LOADS_AHEAD)
            first_r = i - FIRST_MATMUL_LAG
            h_r = i - TRANSPOSE_H_LAG
            second_r = i - SECOND_MATMUL_LAG
            if i - QUANTISE_LAG in grouped_steps:
                quantise_step(i - QUANTISE_LAG)
            if i == SECOND_MATMUL_LAG - 1:
                prepare_wo()
            if i == 0:
                warm_up(WARM_UP)
            if 0 <= h_r < ROUNDS:
                h_bank = transpose_h_round(h_r)
            if i < ROUNDS:
                x_bank = transpose_x_round(i)
            if i < SECOND_MATMUL_LAG:
                warm_up(1)
            if h_r < ROUNDS:
                grouped = work.tile([P, 2 * ROUND_COLS + D], BF16, tag="grouped", align_bytes=64)
                grouped_steps[i] = grouped
                if FIRST_SORTED <= i + 1 < ROUNDS and ROUND_SIZES[i + 1] > SORTED_SUB:
                    sort_x_round(i + 1, grouped[:, 2 * ROUND_COLS :])
            if i < ROUNDS:
                group_round(i, x_bank, grouped, 0)
            if 0 <= h_r < ROUNDS:
                group_round(h_r, h_bank, grouped, 1)
            if i == 0:
                prepare_wg()
            if 0 <= second_r < ROUNDS:
                second_matmul_round(second_r)
            if 0 <= first_r < ROUNDS:
                first_matmul_round(first_r)
            if 0 <= first_r < ROUNDS:
                gate_round(first_r)
            if 0 <= second_r < ROUNDS:
                store_round(second_r)
